import numpy as np
import ml_dtypes

BF16 = ml_dtypes.bfloat16


def bf(x):
    return np.asarray(x, np.float32).astype(BF16)


def f32(x):
    return np.asarray(x, np.float32)


def f64(x):
    return np.asarray(x).astype(np.float64)


def striped(idx):
    return np.tile(idx.reshape(-1, 16).T, (8, 1))


C, S, N, M = 128, 512, 256, 384


def setup_inputs():
    return {"emb": f32(np.random.standard_normal((C, S))), "gamma": f32(1.0 + 0.1 * np.random.standard_normal((C, 1))), "w_qkv": bf(np.random.standard_normal((C, M)) / np.sqrt(C)), "offs": striped(np.random.permutation(np.tile(np.arange(S), 2))[:N])}


def reference(emb, gamma, w_qkv, offs):
    idx = offs[:16].T.reshape(-1)
    x = f64(emb)[:, idx]
    r = np.sqrt(C) / np.sqrt(np.sum(x * x, axis=0, keepdims=True))
    y = x * r * f64(gamma)
    return np.concatenate([x, f64(w_qkv).T @ y], axis=0)

@@ -1,0 +1,52 @@
+import concourse.mybir as mybir
+
+C, S, N, M = 128, 512, 256, 384
+FLOPS = 2 * C * M * N
+
+F32, BF16, U16 = mybir.dt.float32, mybir.dt.bfloat16, mybir.dt.uint16
+MULT = mybir.AluOpType.mult
+COPY = mybir.ActivationFunctionType.Copy
+ABS_RSQRT = mybir.ActivationFunctionType.Abs_reciprocal_sqrt
+
+
+def tile_ringtransformer_kernel(tc, emb, gamma, w_qkv, offs, out):
+    nc = tc.nc
+    with (
+        tc.tile_pool(name="held", bufs=1) as held,
+        tc.psum_pool(name="psum", bufs=1) as psum,
+    ):
+        offsets = held.tile([C, N // 16], U16, name="offsets")
+        nc.sync.dma_start(offsets[:], offs)
+        table = held.tile([C, S], F32, name="table")
+        nc.scalar.dma_start(table[:], emb)
+        weights = held.tile([C, M], BF16, name="weights")
+        nc.gpsimd.dma_start(weights[:], w_qkv)
+        gain = held.tile([C, 1], F32, name="gain")
+        nc.gpsimd.dma_start(gain[:], gamma)
+
+        averager = held.tile([C, C], F32, name="averager")
+        nc.vector.memset(averager[:], 1.0 / C)
+
+        x = held.tile([C, N], F32, name="x")
+        nc.scalar.activation(x[:], table[:].indirect(offsets[:]), COPY)
+        nc.sync.dma_start(out[0:C, :], x[:])
+
+        squares = held.tile([C, N], F32, name="squares")
+        nc.vector.tensor_tensor(squares[:], x[:], x[:], MULT)
+        mean_square = psum.tile([C, N], F32, name="mean_square")
+        nc.tensor.matmul(mean_square[:], averager[:], squares[:], start=True, stop=True)
+        r = held.tile([C, N], F32, name="r")
+        nc.scalar.activation(r[:], mean_square[:], ABS_RSQRT)
+
+        y = held.tile([C, N], BF16, name="y")
+        nc.vector.scalar_tensor_tensor(y[:], x[:], gain[:, 0:1], r[:], MULT, MULT)
+
+        for b in range(M // C):
+            product = psum.tile([C, N], F32, name=f"product{b}")
+            nc.tensor.matmul(product[:], weights[:, b * C : (b + 1) * C], y[:], start=True, stop=True)
+            staged = held.tile([C, N], F32, name=f"staged{b}")
+            if b % 2 == 0:
+                nc.vector.tensor_copy(staged[:], product[:])
+            else:
+                nc.scalar.copy(staged[:], product[:])
+            nc.sync.dma_start(out[C + b * C : C + (b + 1) * C, :], staged[:])

@@ -20,12 +20,15 @@ def tile_ringtransformer_kernel(tc, emb, gamma, w_qkv, offs, out):
         table = held.tile([C, S], F32, name="table")
         nc.scalar.dma_start(table[:], emb)
         weights = held.tile([C, M], BF16, name="weights")
-        nc.gpsimd.dma_start(weights[:], w_qkv)
+        nc.sync.dma_start(weights[:], w_qkv)
         gain = held.tile([C, 1], F32, name="gain")
-        nc.gpsimd.dma_start(gain[:], gamma)
+        nc.sync.dma_start(gain[:], gamma)
 
         averager = held.tile([C, C], F32, name="averager")
         nc.vector.memset(averager[:], 1.0 / C)
+
+        warmed = held.tile([C, 1], F32, name="warmed")
+        nc.scalar.activation(warmed[:], averager[:, 0:1], ABS_RSQRT)
 
         x = held.tile([C, N], F32, name="x")
         nc.scalar.activation(x[:], table[:].indirect(offsets[:]), COPY)

@@ -8,12 +8,17 @@ MULT = mybir.AluOpType.mult
 COPY = mybir.ActivationFunctionType.Copy
 ABS_RSQRT = mybir.ActivationFunctionType.Abs_reciprocal_sqrt
 
+PIECES = 2
+T = N // PIECES
+BLOCKS = M // C
+
 
 def tile_ringtransformer_kernel(tc, emb, gamma, w_qkv, offs, out):
     nc = tc.nc
     with (
         tc.tile_pool(name="held", bufs=1) as held,
-        tc.psum_pool(name="psum", bufs=1) as psum,
+        tc.tile_pool(name="work", bufs=PIECES) as work,
+        tc.psum_pool(name="psum", bufs=PIECES) as psum,
     ):
         offsets = held.tile([C, N // 16], U16, name="offsets")
         nc.sync.dma_start(offsets[:], offs)
@@ -30,26 +35,33 @@ def tile_ringtransformer_kernel(tc, emb, gamma, w_qkv, offs, out):
         warmed = held.tile([C, 1], F32, name="warmed")
         nc.scalar.activation(warmed[:], averager[:, 0:1], ABS_RSQRT)
 
-        x = held.tile([C, N], F32, name="x")
-        nc.scalar.activation(x[:], table[:].indirect(offsets[:]), COPY)
-        nc.sync.dma_start(out[0:C, :], x[:])
 
-        squares = held.tile([C, N], F32, name="squares")
-        nc.vector.tensor_tensor(squares[:], x[:], x[:], MULT)
-        mean_square = psum.tile([C, N], F32, name="mean_square")
-        nc.tensor.matmul(mean_square[:], averager[:], squares[:], start=True, stop=True)
-        r = held.tile([C, N], F32, name="r")
-        nc.scalar.activation(r[:], mean_square[:], ABS_RSQRT)
+        x = [work.tile([C, T], F32, name="x") for p in range(PIECES)]
+        for p in range(PIECES):
+            piece_offsets = offsets[:, p * (T // 16) : (p + 1) * (T // 16)]
+            nc.scalar.activation(x[p][:], table[:].indirect(piece_offsets), COPY)
+            nc.sync.dma_start(out[0:C, p * T : (p + 1) * T], x[p][:])
 
-        y = held.tile([C, N], BF16, name="y")
-        nc.vector.scalar_tensor_tensor(y[:], x[:], gain[:, 0:1], r[:], MULT, MULT)
+        mean_square = [psum.tile([C, T], F32, name="mean_square") for p in range(PIECES)]
+        for p in range(PIECES):
+            squares = work.tile([C, T], F32, name="squares")
+            nc.vector.tensor_tensor(squares[:], x[p][:], x[p][:], MULT)
+            nc.tensor.matmul(mean_square[p][:], averager[:], squares[:], start=True, stop=True)
 
-        for b in range(M // C):
-            product = psum.tile([C, N], F32, name=f"product{b}")
-            nc.tensor.matmul(product[:], weights[:, b * C : (b + 1) * C], y[:], start=True, stop=True)
-            staged = held.tile([C, N], F32, name=f"staged{b}")
-            if b % 2 == 0:
+        y = [work.tile([C, T], BF16, name="y") for p in range(PIECES)]
+        for p in range(PIECES):
+            r = work.tile([C, T], F32, name="r")
+            nc.scalar.activation(r[:], mean_square[p][:], ABS_RSQRT)
+            nc.vector.scalar_tensor_tensor(y[p][:], x[p][:], gain[:, 0:1], r[:], MULT, MULT)
+
+        projected = out[C:, :].rearrange("(b c) j -> c b j", c=C)
+        for p in range(PIECES):
+            product = psum.tile([C, BLOCKS, T], F32, name="product")
+            for b in range(BLOCKS):
+                nc.tensor.matmul(product[:, b, :], weights[:, b * C : (b + 1) * C], y[p][:], start=True, stop=True)
+            staged = work.tile([C, BLOCKS, T], F32, name="staged")
+            if p % 2 == 0:
                 nc.vector.tensor_copy(staged[:], product[:])
             else:
                 nc.scalar.copy(staged[:], product[:])
-            nc.sync.dma_start(out[C + b * C : C + (b + 1) * C, :], staged[:])
+            nc.sync.dma_start(projected[:, :, p * T : (p + 1) * T], staged[:])

@@ -56,12 +56,12 @@ def tile_ringtransformer_kernel(tc, emb, gamma, w_qkv, offs, out):
 
         projected = out[C:, :].rearrange("(b c) j -> c b j", c=C)
         for p in range(PIECES):
-            product = psum.tile([C, BLOCKS, T], F32, name="product")
-            for b in range(BLOCKS):
-                nc.tensor.matmul(product[:, b, :], weights[:, b * C : (b + 1) * C], y[p][:], start=True, stop=True)
             staged = work.tile([C, BLOCKS, T], F32, name="staged")
-            if p % 2 == 0:
-                nc.vector.tensor_copy(staged[:], product[:])
-            else:
-                nc.scalar.copy(staged[:], product[:])
+            for b in range(BLOCKS):
+                product = psum.tile([C, T], F32, name=f"product{b}")
+                nc.tensor.matmul(product[:], weights[:, b * C : (b + 1) * C], y[p][:], start=True, stop=True)
+                if (p * BLOCKS + b) % 2 == 0:
+                    nc.vector.tensor_copy(staged[:, b, :], product[:])
+                else:
+                    nc.scalar.copy(staged[:, b, :], product[:])
             nc.sync.dma_start(projected[:, :, p * T : (p + 1) * T], staged[:])

@@ -10,6 +10,7 @@ ABS_RSQRT = mybir.ActivationFunctionType.Abs_reciprocal_sqrt
 
 PIECES = 2
 T = N // PIECES
+WARM_MATMULS = 6
 BLOCKS = M // C
 
 
@@ -34,6 +35,10 @@ def tile_ringtransformer_kernel(tc, emb, gamma, w_qkv, offs, out):
 
         warmed = held.tile([C, 1], F32, name="warmed")
         nc.scalar.activation(warmed[:], averager[:, 0:1], ABS_RSQRT)
+
+        idle_product = psum.tile([C, C], F32, name="mean_square")
+        for i in range(WARM_MATMULS):
+            nc.tensor.matmul(idle_product[:], averager[:], averager[:], start=True, stop=True)
 
 
         x = [work.tile([C, T], F32, name="x") for p in range(PIECES)]

@@ -59,14 +59,13 @@ def tile_ringtransformer_kernel(tc, emb, gamma, w_qkv, offs, out):
             nc.scalar.activation(r[:], mean_square[p][:], ABS_RSQRT)
             nc.vector.scalar_tensor_tensor(y[p][:], x[p][:], gain[:, 0:1], r[:], MULT, MULT)
 
-        projected = out[C:, :].rearrange("(b c) j -> c b j", c=C)
         for p in range(PIECES):
-            staged = work.tile([C, BLOCKS, T], F32, name="staged")
             for b in range(BLOCKS):
                 product = psum.tile([C, T], F32, name=f"product{b}")
                 nc.tensor.matmul(product[:], weights[:, b * C : (b + 1) * C], y[p][:], start=True, stop=True)
+                staged = work.tile([C, T], F32, name=f"staged{b}")
                 if (p * BLOCKS + b) % 2 == 0:
-                    nc.vector.tensor_copy(staged[:, b, :], product[:])
+                    nc.vector.tensor_copy(staged[:], product[:])
                 else:
-                    nc.scalar.copy(staged[:, b, :], product[:])
-            nc.sync.dma_start(projected[:, :, p * T : (p + 1) * T], staged[:])
+                    nc.scalar.copy(staged[:], product[:])
+                nc.sync.dma_start(out[C + b * C : C + (b + 1) * C, p * T : (p + 1) * T], staged[:])

@@ -26,9 +26,9 @@ def tile_ringtransformer_kernel(tc, emb, gamma, w_qkv, offs, out):
         table = held.tile([C, S], F32, name="table")
         nc.scalar.dma_start(table[:], emb)
         weights = held.tile([C, M], BF16, name="weights")
-        nc.sync.dma_start(weights[:], w_qkv)
+        nc.scalar.dma_start(weights[:], w_qkv)
         gain = held.tile([C, 1], F32, name="gain")
-        nc.sync.dma_start(gain[:], gamma)
+        nc.scalar.dma_start(gain[:], gamma)
 
         averager = held.tile([C, C], F32, name="averager")
         nc.vector.memset(averager[:], 1.0 / C)
@@ -41,31 +41,33 @@ def tile_ringtransformer_kernel(tc, emb, gamma, w_qkv, offs, out):
             nc.tensor.matmul(idle_product[:], averager[:], averager[:], start=True, stop=True)
 
 
-        x = [work.tile([C, T], F32, name="x") for p in range(PIECES)]
+        whole_x = held.tile([C, N], F32, name="whole_x")
+        x = [whole_x[:, p * T : (p + 1) * T] for p in range(PIECES)]
         for p in range(PIECES):
             piece_offsets = offsets[:, p * (T // 16) : (p + 1) * (T // 16)]
-            nc.scalar.activation(x[p][:], table[:].indirect(piece_offsets), COPY)
-            nc.sync.dma_start(out[0:C, p * T : (p + 1) * T], x[p][:])
+            nc.scalar.activation(x[p], table[:].indirect(piece_offsets), COPY)
+        nc.sync.dma_start(out[0:C, :], whole_x[:])
 
         mean_square = [psum.tile([C, T], F32, name="mean_square") for p in range(PIECES)]
         for p in range(PIECES):
             squares = work.tile([C, T], F32, name="squares")
-            nc.vector.tensor_tensor(squares[:], x[p][:], x[p][:], MULT)
+            nc.vector.tensor_tensor(squares[:], x[p], x[p], MULT)
             nc.tensor.matmul(mean_square[p][:], averager[:], squares[:], start=True, stop=True)
 
         y = [work.tile([C, T], BF16, name="y") for p in range(PIECES)]
         for p in range(PIECES):
             r = work.tile([C, T], F32, name="r")
             nc.scalar.activation(r[:], mean_square[p][:], ABS_RSQRT)
-            nc.vector.scalar_tensor_tensor(y[p][:], x[p][:], gain[:, 0:1], r[:], MULT, MULT)
+            nc.vector.scalar_tensor_tensor(y[p][:], x[p], gain[:, 0:1], r[:], MULT, MULT)
 
+        projected = out[C:, :].rearrange("(b c) j -> c b j", c=C)
         for p in range(PIECES):
+            staged = work.tile([C, BLOCKS, T], F32, name="staged")
             for b in range(BLOCKS):
                 product = psum.tile([C, T], F32, name=f"product{b}")
                 nc.tensor.matmul(product[:], weights[:, b * C : (b + 1) * C], y[p][:], start=True, stop=True)
-                staged = work.tile([C, T], F32, name=f"staged{b}")
                 if (p * BLOCKS + b) % 2 == 0:
-                    nc.vector.tensor_copy(staged[:], product[:])
+                    nc.vector.tensor_copy(staged[:, b, :], product[:])
                 else:
-                    nc.scalar.copy(staged[:], product[:])
-                nc.sync.dma_start(out[C + b * C : C + (b + 1) * C, p * T : (p + 1) * T], staged[:])
+                    nc.scalar.copy(staged[:, b, :], product[:])
+            nc.sync.dma_start(projected[:, :, p * T : (p + 1) * T], staged[:])

@@ -10,8 +10,8 @@ ABS_RSQRT = mybir.ActivationFunctionType.Abs_reciprocal_sqrt
 
 PIECES = 2
 T = N // PIECES
-WARM_MATMULS = 6
 BLOCKS = M // C
+WARM_MATMULS = 6
 
 
 def tile_ringtransformer_kernel(tc, emb, gamma, w_qkv, offs, out):
@@ -21,44 +21,45 @@ def tile_ringtransformer_kernel(tc, emb, gamma, w_qkv, offs, out):
         tc.tile_pool(name="work", bufs=PIECES) as work,
         tc.psum_pool(name="psum", bufs=PIECES) as psum,
     ):
+        one = held.tile([C, 1], F32, name="one")
+        nc.vector.memset(one[:], 1.0)
+        warmed = held.tile([C, 1], F32, name="warmed")
+        nc.scalar.activation(warmed[:], one[:], ABS_RSQRT)
+
         offsets = held.tile([C, N // 16], U16, name="offsets")
         nc.sync.dma_start(offsets[:], offs)
         table = held.tile([C, S], F32, name="table")
-        nc.scalar.dma_start(table[:], emb)
+        nc.sync.dma_start(table[:], emb)
         weights = held.tile([C, M], BF16, name="weights")
-        nc.scalar.dma_start(weights[:], w_qkv)
+        nc.sync.dma_start(weights[:], w_qkv)
         gain = held.tile([C, 1], F32, name="gain")
-        nc.scalar.dma_start(gain[:], gamma)
+        nc.sync.dma_start(gain[:], gamma)
 
         averager = held.tile([C, C], F32, name="averager")
         nc.vector.memset(averager[:], 1.0 / C)
-
-        warmed = held.tile([C, 1], F32, name="warmed")
-        nc.scalar.activation(warmed[:], averager[:, 0:1], ABS_RSQRT)
 
         idle_product = psum.tile([C, C], F32, name="mean_square")
         for i in range(WARM_MATMULS):
             nc.tensor.matmul(idle_product[:], averager[:], averager[:], start=True, stop=True)
 
 
-        whole_x = held.tile([C, N], F32, name="whole_x")
-        x = [whole_x[:, p * T : (p + 1) * T] for p in range(PIECES)]
+        x = [work.tile([C, T], F32, name="x") for p in range(PIECES)]
         for p in range(PIECES):
             piece_offsets = offsets[:, p * (T // 16) : (p + 1) * (T // 16)]
-            nc.scalar.activation(x[p], table[:].indirect(piece_offsets), COPY)
-        nc.sync.dma_start(out[0:C, :], whole_x[:])
+            nc.scalar.activation(x[p][:], table[:].indirect(piece_offsets), COPY)
+            nc.sync.dma_start(out[0:C, p * T : (p + 1) * T], x[p][:])
 
         mean_square = [psum.tile([C, T], F32, name="mean_square") for p in range(PIECES)]
         for p in range(PIECES):
             squares = work.tile([C, T], F32, name="squares")
-            nc.vector.tensor_tensor(squares[:], x[p], x[p], MULT)
+            nc.vector.tensor_tensor(squares[:], x[p][:], x[p][:], MULT)
             nc.tensor.matmul(mean_square[p][:], averager[:], squares[:], start=True, stop=True)
 
         y = [work.tile([C, T], BF16, name="y") for p in range(PIECES)]
         for p in range(PIECES):
             r = work.tile([C, T], F32, name="r")
             nc.scalar.activation(r[:], mean_square[p][:], ABS_RSQRT)
-            nc.vector.scalar_tensor_tensor(y[p][:], x[p], gain[:, 0:1], r[:], MULT, MULT)
+            nc.vector.scalar_tensor_tensor(y[p][:], x[p][:], gain[:, 0:1], r[:], MULT, MULT)
 
         projected = out[C:, :].rearrange("(b c) j -> c b j", c=C)
         for p in range(PIECES):

@@ -11,7 +11,7 @@ ABS_RSQRT = mybir.ActivationFunctionType.Abs_reciprocal_sqrt
 PIECES = 2
 T = N // PIECES
 BLOCKS = M // C
-WARM_MATMULS = 6
+WARM_MATMULS = 4
 
 
 def tile_ringtransformer_kernel(tc, emb, gamma, w_qkv, offs, out):

@@ -8,8 +8,15 @@ MULT = mybir.AluOpType.mult
 COPY = mybir.ActivationFunctionType.Copy
 ABS_RSQRT = mybir.ActivationFunctionType.Abs_reciprocal_sqrt
 
-PIECES = 2
-T = N // PIECES
+WIDTHS = (64, 64, 64, 64)
+assert sum(WIDTHS) == N and all(width % 32 == 0 for width in WIDTHS)
+PIECES = len(WIDTHS)
+BOUNDS = [(sum(WIDTHS[:p]), sum(WIDTHS[: p + 1])) for p in range(PIECES)]
+WIDEST = C
+assert max(WIDTHS) <= WIDEST
+STORES = 2
+H = N // STORES
+BANKS = 8
 BLOCKS = M // C
 WARM_MATMULS = 4
 
@@ -19,7 +26,7 @@ def tile_ringtransformer_kernel(tc, emb, gamma, w_qkv, offs, out):
     with (
         tc.tile_pool(name="held", bufs=1) as held,
         tc.tile_pool(name="work", bufs=PIECES) as work,
-        tc.psum_pool(name="psum", bufs=PIECES) as psum,
+        tc.psum_pool(name="psum", bufs=BANKS) as psum,
     ):
         one = held.tile([C, 1], F32, name="one")
         nc.vector.memset(one[:], 1.0)
@@ -38,37 +45,39 @@ def tile_ringtransformer_kernel(tc, emb, gamma, w_qkv, offs, out):
         averager = held.tile([C, C], F32, name="averager")
         nc.vector.memset(averager[:], 1.0 / C)
 
-        idle_product = psum.tile([C, C], F32, name="mean_square")
+        idle_product = psum.tile([C, WIDEST], F32, name="bank")
         for i in range(WARM_MATMULS):
-            nc.tensor.matmul(idle_product[:], averager[:], averager[:], start=True, stop=True)
+            nc.tensor.matmul(idle_product[:, 0:C], averager[:], averager[:], start=True, stop=True)
 
 
-        x = [work.tile([C, T], F32, name="x") for p in range(PIECES)]
-        for p in range(PIECES):
-            piece_offsets = offsets[:, p * (T // 16) : (p + 1) * (T // 16)]
-            nc.scalar.activation(x[p][:], table[:].indirect(piece_offsets), COPY)
-            nc.sync.dma_start(out[0:C, p * T : (p + 1) * T], x[p][:])
+        x = held.tile([C, N], F32, name="x")
+        for lo, hi in BOUNDS:
+            nc.scalar.activation(x[:, lo:hi], table[:].indirect(offsets[:, lo // 16 : hi // 16]), COPY)
+        for s in range(STORES):
+            nc.sync.dma_start(out[0:C, s * H : (s + 1) * H], x[:, s * H : (s + 1) * H])
 
-        mean_square = [psum.tile([C, T], F32, name="mean_square") for p in range(PIECES)]
-        for p in range(PIECES):
-            squares = work.tile([C, T], F32, name="squares")
-            nc.vector.tensor_tensor(squares[:], x[p][:], x[p][:], MULT)
-            nc.tensor.matmul(mean_square[p][:], averager[:], squares[:], start=True, stop=True)
+        mean_square = []
+        for lo, hi in BOUNDS:
+            squares = work.tile([C, WIDEST], F32, name="squares")
+            nc.vector.tensor_tensor(squares[:, 0 : hi - lo], x[:, lo:hi], x[:, lo:hi], MULT)
+            mean_square.append(psum.tile([C, WIDEST], F32, name="bank"))
+            nc.tensor.matmul(mean_square[-1][:, 0 : hi - lo], averager[:], squares[:, 0 : hi - lo], start=True, stop=True)
 
-        y = [work.tile([C, T], BF16, name="y") for p in range(PIECES)]
-        for p in range(PIECES):
-            r = work.tile([C, T], F32, name="r")
-            nc.scalar.activation(r[:], mean_square[p][:], ABS_RSQRT)
-            nc.vector.scalar_tensor_tensor(y[p][:], x[p][:], gain[:, 0:1], r[:], MULT, MULT)
+        y = held.tile([C, N], BF16, name="y")
+        for p, (lo, hi) in enumerate(BOUNDS):
+            r = work.tile([C, WIDEST], F32, name="r")
+            nc.scalar.activation(r[:, 0 : hi - lo], mean_square[p][:, 0 : hi - lo], ABS_RSQRT)
+            nc.vector.scalar_tensor_tensor(y[:, lo:hi], x[:, lo:hi], gain[:, 0:1], r[:, 0 : hi - lo], MULT, MULT)
 
-        projected = out[C:, :].rearrange("(b c) j -> c b j", c=C)
-        for p in range(PIECES):
-            staged = work.tile([C, BLOCKS, T], F32, name="staged")
+        staged = held.tile([C, BLOCKS, N], F32, name="staged")
+        for p, (lo, hi) in enumerate(BOUNDS):
             for b in range(BLOCKS):
-                product = psum.tile([C, T], F32, name=f"product{b}")
-                nc.tensor.matmul(product[:], weights[:, b * C : (b + 1) * C], y[p][:], start=True, stop=True)
+                product = psum.tile([C, WIDEST], F32, name="bank")
+                nc.tensor.matmul(product[:, 0 : hi - lo], weights[:, b * C : (b + 1) * C], y[:, lo:hi], start=True, stop=True)
                 if (p * BLOCKS + b) % 2 == 0:
-                    nc.vector.tensor_copy(staged[:, b, :], product[:])
+                    nc.vector.tensor_copy(staged[:, b, lo:hi], product[:, 0 : hi - lo])
                 else:
-                    nc.scalar.copy(staged[:, b, :], product[:])
-            nc.sync.dma_start(projected[:, :, p * T : (p + 1) * T], staged[:])
+                    nc.scalar.copy(staged[:, b, lo:hi], product[:, 0 : hi - lo])
+        projected = out[C:, :].rearrange("(b c) j -> c b j", c=C)
+        for s in range(STORES):
+            nc.sync.dma_start(projected[:, :, s * H : (s + 1) * H], staged[:, :, s * H : (s + 1) * H])

import concourse.mybir as mybir

C, S, N, M = 128, 512, 256, 384
FLOPS = 2 * C * M * N

F32, BF16, U16 = mybir.dt.float32, mybir.dt.bfloat16, mybir.dt.uint16
MULT = mybir.AluOpType.mult
COPY = mybir.ActivationFunctionType.Copy
ABS_RSQRT = mybir.ActivationFunctionType.Abs_reciprocal_sqrt

WIDTHS = (64, 64, 64, 64)
assert sum(WIDTHS) == N and all(width % 32 == 0 for width in WIDTHS)
PIECES = len(WIDTHS)
BOUNDS = [(sum(WIDTHS[:p]), sum(WIDTHS[: p + 1])) for p in range(PIECES)]
WIDEST = C
assert max(WIDTHS) <= WIDEST
STORES = 2
H = N // STORES
BANKS = 8
BLOCKS = M // C
WARM_MATMULS = 4


def tile_ringtransformer_kernel(tc, emb, gamma, w_qkv, offs, out):
    nc = tc.nc
    with (
        tc.tile_pool(name="held", bufs=1) as held,
        tc.tile_pool(name="work", bufs=PIECES) as work,
        tc.psum_pool(name="psum", bufs=BANKS) as psum,
    ):
        one = held.tile([C, 1], F32, name="one")
        nc.vector.memset(one[:], 1.0)
        warmed = held.tile([C, 1], F32, name="warmed")
        nc.scalar.activation(warmed[:], one[:], ABS_RSQRT)

        offsets = held.tile([C, N // 16], U16, name="offsets")
        nc.sync.dma_start(offsets[:], offs)
        table = held.tile([C, S], F32, name="table")
        nc.sync.dma_start(table[:], emb)
        weights = held.tile([C, M], BF16, name="weights")
        nc.sync.dma_start(weights[:], w_qkv)
        gain = held.tile([C, 1], F32, name="gain")
        nc.sync.dma_start(gain[:], gamma)

        averager = held.tile([C, C], F32, name="averager")
        nc.vector.memset(averager[:], 1.0 / C)

        idle_product = psum.tile([C, WIDEST], F32, name="bank")
        for i in range(WARM_MATMULS):
            nc.tensor.matmul(idle_product[:, 0:C], averager[:], averager[:], start=True, stop=True)


        x = held.tile([C, N], F32, name="x")
        for lo, hi in BOUNDS:
            nc.scalar.activation(x[:, lo:hi], table[:].indirect(offsets[:, lo // 16 : hi // 16]), COPY)
        for s in range(STORES):
            nc.sync.dma_start(out[0:C, s * H : (s + 1) * H], x[:, s * H : (s + 1) * H])

        mean_square = []
        for lo, hi in BOUNDS:
            squares = work.tile([C, WIDEST], F32, name="squares")
            nc.vector.tensor_tensor(squares[:, 0 : hi - lo], x[:, lo:hi], x[:, lo:hi], MULT)
            mean_square.append(psum.tile([C, WIDEST], F32, name="bank"))
            nc.tensor.matmul(mean_square[-1][:, 0 : hi - lo], averager[:], squares[:, 0 : hi - lo], start=True, stop=True)

        y = held.tile([C, N], BF16, name="y")
        for p, (lo, hi) in enumerate(BOUNDS):
            r = work.tile([C, WIDEST], F32, name="r")
            nc.scalar.activation(r[:, 0 : hi - lo], mean_square[p][:, 0 : hi - lo], ABS_RSQRT)
            nc.vector.scalar_tensor_tensor(y[:, lo:hi], x[:, lo:hi], gain[:, 0:1], r[:, 0 : hi - lo], MULT, MULT)

        staged = held.tile([C, BLOCKS, N], F32, name="staged")
        for p, (lo, hi) in enumerate(BOUNDS):
            for b in range(BLOCKS):
                product = psum.tile([C, WIDEST], F32, name="bank")
                nc.tensor.matmul(product[:, 0 : hi - lo], weights[:, b * C : (b + 1) * C], y[:, lo:hi], start=True, stop=True)
                if (p * BLOCKS + b) % 2 == 0:
                    nc.vector.tensor_copy(staged[:, b, lo:hi], product[:, 0 : hi - lo])
                else:
                    nc.scalar.copy(staged[:, b, lo:hi], product[:, 0 : hi - lo])
        projected = out[C:, :].rearrange("(b c) j -> c b j", c=C)
        for s in range(STORES):
            nc.sync.dma_start(projected[:, :, s * H : (s + 1) * H], staged[:, :, s * H : (s + 1) * H])
